import numpy as np
import ml_dtypes

BF16 = ml_dtypes.bfloat16


def bf(x):
    return np.asarray(x, np.float32).astype(BF16)


def f32(x):
    return np.asarray(x, np.float32)


def f64(x):
    return np.asarray(x).astype(np.float64)


def striped(idx):
    return np.tile(idx.reshape(-1, 16).T, (8, 1))


D, BD, K, N = 256, 128, 1024, 2048


def sigmoid(v):
    return 1.0 / (1.0 + np.exp(-v))


def setup_inputs():
    return {"splat": bf(np.random.standard_normal((BD, K))), "dec_w": bf(np.random.standard_normal((BD, D)) / np.sqrt(BD)), "dec_b": f32(0.1 * np.random.standard_normal((D, 1))), "tok": bf(np.random.standard_normal((D, N))), "gate_w": bf(np.random.standard_normal((D, D)) / np.sqrt(D)), "gate_b": f32(0.1 * np.random.standard_normal((D, 1))), "offs": striped(np.random.permutation(np.tile(np.arange(K), 2))[:N])}


def reference(splat, dec_w, dec_b, tok, gate_w, gate_b, offs):
    idx = offs[:16].T.reshape(-1)
    flow = f64(dec_w).T @ f64(splat)[:, idx] + f64(dec_b)
    gate = sigmoid(f64(gate_w).T @ f64(tok) + f64(gate_b))
    return flow * gate

@@ -1,0 +1,84 @@
+import concourse.mybir as mybir
+
+BF16, F32, U16 = mybir.dt.bfloat16, mybir.dt.float32, mybir.dt.uint16
+ADD, MULT = mybir.AluOpType.add, mybir.AluOpType.mult
+SIGMOID = mybir.ActivationFunctionType.Sigmoid
+
+P = 128
+BOTTLENECK = 128
+SPLATS = 1024
+FEATURES = 256
+TOKENS = 2048
+PIECE = 512
+BLOCKS = FEATURES // P
+PIECES = TOKENS // PIECE
+PIECE_OFFSET_COLUMNS = PIECE // 16
+PSUM_BANKS = 8
+
+FLOPS = 2 * TOKENS * FEATURES * (BOTTLENECK + FEATURES)
+
+
+def tile_splatinformationflow_kernel(tc, splat, dec_w, dec_b, tok, gate_w, gate_b, offs, out):
+    nc = tc.nc
+    output_tiles = [(piece, block) for piece in range(PIECES) for block in range(BLOCKS)]
+
+    with (
+        tc.tile_pool(name="held", bufs=1) as held,
+        tc.tile_pool(name="work", bufs=len(output_tiles)) as work,
+        tc.psum_pool(name="psum", bufs=PSUM_BANKS) as psum,
+    ):
+        gate_w_sb = held.tile([P, BLOCKS, FEATURES], BF16, name="gate_w_sb")
+        nc.sync.dma_start(gate_w_sb[:], gate_w.rearrange("(half p) m -> p half m", p=P))
+
+        tok_view = tok.rearrange("(half p) j -> p half j", p=P)
+        tok_sb = []
+        for piece in range(PIECES):
+            tok_piece = held.tile([P, BLOCKS, PIECE], BF16, name=f"tok_piece{piece}")
+            queue = nc.scalar if piece % 2 == 0 else nc.sync
+            queue.dma_start(tok_piece[:], tok_view[:, :, piece * PIECE : (piece + 1) * PIECE])
+            tok_sb.append(tok_piece)
+
+        gate_b_sb = held.tile([P, BLOCKS], F32, name="gate_b_sb")
+        dec_b_sb = held.tile([P, BLOCKS], F32, name="dec_b_sb")
+        table = held.tile([BOTTLENECK, SPLATS], BF16, name="table")
+        dec_w_sb = held.tile([BOTTLENECK, FEATURES], BF16, name="dec_w_sb")
+        with nc.allow_non_contiguous_dma(reason="a bias vector, one element to a partition"):
+            nc.gpsimd.dma_start(gate_b_sb[:], gate_b.rearrange("(block p) one -> p (block one)", p=P))
+        nc.gpsimd.dma_start(table[:], splat)
+        nc.gpsimd.dma_start(dec_w_sb[:], dec_w)
+        with nc.allow_non_contiguous_dma(reason="a bias vector, one element to a partition"):
+            nc.gpsimd.dma_start(dec_b_sb[:], dec_b.rearrange("(block p) one -> p (block one)", p=P))
+
+        offsets = held.tile([P, TOKENS // 16], U16, name="offsets")
+        nc.sync.dma_start(offsets[:], offs)
+
+        gates = {}
+        for piece, block in output_tiles:
+            gate_acc = psum.tile([P, PIECE], F32, name="gate_acc", tag="bank")
+            for half in range(BLOCKS):
+                nc.tensor.matmul(
+                    gate_acc[:],
+                    gate_w_sb[:, half, block * P : (block + 1) * P],
+                    tok_sb[piece][:, half, :],
+                    start=(half == 0),
+                    stop=(half == BLOCKS - 1),
+                )
+            gate = work.tile([P, PIECE], F32, name="gate")
+            nc.scalar.activation(gate[:], gate_acc[:], SIGMOID, bias=gate_b_sb[:, block : block + 1], scale=1.0)
+            gates[piece, block] = gate
+
+        for piece, block in output_tiles:
+            piece_offsets = offsets[:, piece * PIECE_OFFSET_COLUMNS : (piece + 1) * PIECE_OFFSET_COLUMNS]
+            flow_acc = psum.tile([P, PIECE], F32, name="flow_acc", tag="bank")
+            nc.tensor.matmul(
+                flow_acc[:],
+                dec_w_sb[:, block * P : (block + 1) * P],
+                table[:].indirect(piece_offsets),
+                start=True,
+                stop=True,
+            )
+            result = work.tile([P, PIECE], F32, name="result")
+            nc.vector.scalar_tensor_tensor(
+                result[:], flow_acc[:], dec_b_sb[:, block : block + 1], gates[piece, block][:], ADD, MULT
+            )
+            nc.sync.dma_start(out[block * P : (block + 1) * P, piece * PIECE : (piece + 1) * PIECE], result[:])

@@ -11,6 +11,7 @@ FEATURES = 256
 TOKENS = 2048
 PIECE = 512
 BLOCKS = FEATURES // P
+HALVES = FEATURES // P
 PIECES = TOKENS // PIECE
 PIECE_OFFSET_COLUMNS = PIECE // 16
 PSUM_BANKS = 8
@@ -27,41 +28,44 @@ def tile_splatinformationflow_kernel(tc, splat, dec_w, dec_b, tok, gate_w, gate_
         tc.tile_pool(name="work", bufs=len(output_tiles)) as work,
         tc.psum_pool(name="psum", bufs=PSUM_BANKS) as psum,
     ):
-        gate_w_sb = held.tile([P, BLOCKS, FEATURES], BF16, name="gate_w_sb")
-        nc.sync.dma_start(gate_w_sb[:], gate_w.rearrange("(half p) m -> p half m", p=P))
-
-        tok_view = tok.rearrange("(half p) j -> p half j", p=P)
-        tok_sb = []
-        for piece in range(PIECES):
-            tok_piece = held.tile([P, BLOCKS, PIECE], BF16, name=f"tok_piece{piece}")
-            queue = nc.scalar if piece % 2 == 0 else nc.sync
-            queue.dma_start(tok_piece[:], tok_view[:, :, piece * PIECE : (piece + 1) * PIECE])
-            tok_sb.append(tok_piece)
-
+        queues = [nc.sync, nc.scalar]
+        gate_w_sb = [held.tile([P, FEATURES], BF16, name=f"gate_w_half{half}") for half in range(HALVES)]
+        tok_sb = [
+            [held.tile([P, PIECE], BF16, name=f"tok_piece{piece}_half{half}") for half in range(HALVES)]
+            for piece in range(PIECES)
+        ]
         gate_b_sb = held.tile([P, BLOCKS], F32, name="gate_b_sb")
         dec_b_sb = held.tile([P, BLOCKS], F32, name="dec_b_sb")
         table = held.tile([BOTTLENECK, SPLATS], BF16, name="table")
         dec_w_sb = held.tile([BOTTLENECK, FEATURES], BF16, name="dec_w_sb")
-        with nc.allow_non_contiguous_dma(reason="a bias vector, one element to a partition"):
-            nc.gpsimd.dma_start(gate_b_sb[:], gate_b.rearrange("(block p) one -> p (block one)", p=P))
-        nc.gpsimd.dma_start(table[:], splat)
-        nc.gpsimd.dma_start(dec_w_sb[:], dec_w)
-        with nc.allow_non_contiguous_dma(reason="a bias vector, one element to a partition"):
-            nc.gpsimd.dma_start(dec_b_sb[:], dec_b.rearrange("(block p) one -> p (block one)", p=P))
-
         offsets = held.tile([P, TOKENS // 16], U16, name="offsets")
+
+        for half in range(HALVES):
+            queues[half].dma_start(gate_w_sb[half][:], gate_w[half * P : (half + 1) * P, :])
+        for piece in range(PIECES):
+            for half in range(HALVES):
+                queues[half].dma_start(
+                    tok_sb[piece][half][:], tok[half * P : (half + 1) * P, piece * PIECE : (piece + 1) * PIECE]
+                )
+            if piece == 0:
+                with nc.allow_non_contiguous_dma(reason="a bias vector, one element to a partition"):
+                    nc.scalar.dma_start(gate_b_sb[:], gate_b.rearrange("(block p) one -> p (block one)", p=P))
         nc.sync.dma_start(offsets[:], offs)
+        nc.scalar.dma_start(dec_w_sb[:], dec_w)
+        nc.sync.dma_start(table[:], splat)
+        with nc.allow_non_contiguous_dma(reason="a bias vector, one element to a partition"):
+            nc.scalar.dma_start(dec_b_sb[:], dec_b.rearrange("(block p) one -> p (block one)", p=P))
 
         gates = {}
         for piece, block in output_tiles:
             gate_acc = psum.tile([P, PIECE], F32, name="gate_acc", tag="bank")
-            for half in range(BLOCKS):
+            for half in range(HALVES):
                 nc.tensor.matmul(
                     gate_acc[:],
-                    gate_w_sb[:, half, block * P : (block + 1) * P],
-                    tok_sb[piece][:, half, :],
+                    gate_w_sb[half][:, block * P : (block + 1) * P],
+                    tok_sb[piece][half][:],
                     start=(half == 0),
-                    stop=(half == BLOCKS - 1),
+                    stop=(half == HALVES - 1),
                 )
             gate = work.tile([P, PIECE], F32, name="gate")
             nc.scalar.activation(gate[:], gate_acc[:], SIGMOID, bias=gate_b_sb[:, block : block + 1], scale=1.0)

@@ -15,6 +15,7 @@ HALVES = FEATURES // P
 PIECES = TOKENS // PIECE
 PIECE_OFFSET_COLUMNS = PIECE // 16
 PSUM_BANKS = 8
+WARMUP_MATMULS = 6
 
 FLOPS = 2 * TOKENS * FEATURES * (BOTTLENECK + FEATURES)
 
@@ -55,6 +56,12 @@ def tile_splatinformationflow_kernel(tc, splat, dec_w, dec_b, tok, gate_w, gate_
         nc.sync.dma_start(table[:], splat)
         with nc.allow_non_contiguous_dma(reason="a bias vector, one element to a partition"):
             nc.scalar.dma_start(dec_b_sb[:], dec_b.rearrange("(block p) one -> p (block one)", p=P))
+
+        zeros = held.tile([P, PIECE], BF16, name="zeros")
+        nc.vector.memset(zeros[:], 0.0)
+        warm_acc = psum.tile([P, PIECE], F32, name="warm_acc", tag="bank")
+        for repeat in range(WARMUP_MATMULS):
+            nc.tensor.matmul(warm_acc[:], zeros[:, 0:P], zeros[:], start=True, stop=True)
 
         gates = {}
         for piece, block in output_tiles:

@@ -15,7 +15,7 @@ HALVES = FEATURES // P
 PIECES = TOKENS // PIECE
 PIECE_OFFSET_COLUMNS = PIECE // 16
 PSUM_BANKS = 8
-WARMUP_MATMULS = 6
+WARMUP_MATMULS = 12
 
 FLOPS = 2 * TOKENS * FEATURES * (BOTTLENECK + FEATURES)
 
@@ -57,11 +57,11 @@ def tile_splatinformationflow_kernel(tc, splat, dec_w, dec_b, tok, gate_w, gate_
         with nc.allow_non_contiguous_dma(reason="a bias vector, one element to a partition"):
             nc.scalar.dma_start(dec_b_sb[:], dec_b.rearrange("(block p) one -> p (block one)", p=P))
 
-        zeros = held.tile([P, PIECE], BF16, name="zeros")
+        zeros = held.tile([P, P], BF16, name="zeros")
         nc.vector.memset(zeros[:], 0.0)
-        warm_acc = psum.tile([P, PIECE], F32, name="warm_acc", tag="bank")
+        warm_acc = psum.tile([P, P], F32, name="warm_acc", tag="bank")
         for repeat in range(WARMUP_MATMULS):
-            nc.tensor.matmul(warm_acc[:], zeros[:, 0:P], zeros[:], start=True, stop=True)
+            nc.tensor.matmul(warm_acc[:], zeros[:], zeros[:], start=True, stop=True)
 
         gates = {}
         for piece, block in output_tiles:

@@ -15,7 +15,7 @@ HALVES = FEATURES // P
 PIECES = TOKENS // PIECE
 PIECE_OFFSET_COLUMNS = PIECE // 16
 PSUM_BANKS = 8
-WARMUP_MATMULS = 12
+WARMUP_MATMULS = 8
 
 FLOPS = 2 * TOKENS * FEATURES * (BOTTLENECK + FEATURES)
 
@@ -41,21 +41,24 @@ def tile_splatinformationflow_kernel(tc, splat, dec_w, dec_b, tok, gate_w, gate_
         dec_w_sb = held.tile([BOTTLENECK, FEATURES], BF16, name="dec_w_sb")
         offsets = held.tile([P, TOKENS // 16], U16, name="offsets")
 
+        def tok_part(piece, half):
+            return tok[half * P : (half + 1) * P, piece * PIECE : (piece + 1) * PIECE]
+
+        loads = []
         for half in range(HALVES):
-            queues[half].dma_start(gate_w_sb[half][:], gate_w[half * P : (half + 1) * P, :])
-        for piece in range(PIECES):
+            loads.append((gate_w_sb[half], gate_w[half * P : (half + 1) * P, :]))
+            loads.append((tok_sb[0][half], tok_part(0, half)))
+        loads.append((gate_b_sb, gate_b.rearrange("(block p) one -> p (block one)", p=P)))
+        for piece in range(1, PIECES):
             for half in range(HALVES):
-                queues[half].dma_start(
-                    tok_sb[piece][half][:], tok[half * P : (half + 1) * P, piece * PIECE : (piece + 1) * PIECE]
-                )
-            if piece == 0:
-                with nc.allow_non_contiguous_dma(reason="a bias vector, one element to a partition"):
-                    nc.scalar.dma_start(gate_b_sb[:], gate_b.rearrange("(block p) one -> p (block one)", p=P))
-        nc.sync.dma_start(offsets[:], offs)
-        nc.scalar.dma_start(dec_w_sb[:], dec_w)
-        nc.sync.dma_start(table[:], splat)
-        with nc.allow_non_contiguous_dma(reason="a bias vector, one element to a partition"):
-            nc.scalar.dma_start(dec_b_sb[:], dec_b.rearrange("(block p) one -> p (block one)", p=P))
+                loads.append((tok_sb[piece][half], tok_part(piece, half)))
+        loads.append((dec_w_sb, dec_w))
+        loads.append((offsets, offs))
+        loads.append((table, splat))
+        loads.append((dec_b_sb, dec_b.rearrange("(block p) one -> p (block one)", p=P)))
+        with nc.allow_non_contiguous_dma(reason="the bias vectors: one element to a partition"):
+            for position, (destination, source) in enumerate(loads):
+                queues[position % len(queues)].dma_start(destination[:], source)
 
         zeros = held.tile([P, P], BF16, name="zeros")
         nc.vector.memset(zeros[:], 0.0)
@@ -64,19 +67,23 @@ def tile_splatinformationflow_kernel(tc, splat, dec_w, dec_b, tok, gate_w, gate_
             nc.tensor.matmul(warm_acc[:], zeros[:], zeros[:], start=True, stop=True)
 
         gates = {}
-        for piece, block in output_tiles:
-            gate_acc = psum.tile([P, PIECE], F32, name="gate_acc", tag="bank")
+        for piece in range(PIECES):
+            gate_accs = [psum.tile([P, PIECE], F32, name=f"gate_acc_block{block}", tag="bank") for block in range(BLOCKS)]
             for half in range(HALVES):
-                nc.tensor.matmul(
-                    gate_acc[:],
-                    gate_w_sb[half][:, block * P : (block + 1) * P],
-                    tok_sb[piece][half][:],
-                    start=(half == 0),
-                    stop=(half == HALVES - 1),
+                for block in range(BLOCKS):
+                    nc.tensor.matmul(
+                        gate_accs[block][:],
+                        gate_w_sb[half][:, block * P : (block + 1) * P],
+                        tok_sb[piece][half][:],
+                        start=(half == 0),
+                        stop=(half == HALVES - 1),
+                    )
+            for block in range(BLOCKS):
+                gate = work.tile([P, PIECE], F32, name="gate")
+                nc.scalar.activation(
+                    gate[:], gate_accs[block][:], SIGMOID, bias=gate_b_sb[:, block : block + 1], scale=1.0
                 )
-            gate = work.tile([P, PIECE], F32, name="gate")
-            nc.scalar.activation(gate[:], gate_acc[:], SIGMOID, bias=gate_b_sb[:, block : block + 1], scale=1.0)
-            gates[piece, block] = gate
+                gates[piece, block] = gate
 
         for piece, block in output_tiles:
             piece_offsets = offsets[:, piece * PIECE_OFFSET_COLUMNS : (piece + 1) * PIECE_OFFSET_COLUMNS]

@@ -13,8 +13,10 @@ PIECE = 512
 BLOCKS = FEATURES // P
 HALVES = FEATURES // P
 PIECES = TOKENS // PIECE
+LAST_PIECE = PIECES - 1
 PIECE_OFFSET_COLUMNS = PIECE // 16
 PSUM_BANKS = 8
+CHUNK = 64
 WARMUP_MATMULS = 8
 
 FLOPS = 2 * TOKENS * FEATURES * (BOTTLENECK + FEATURES)
@@ -22,11 +24,10 @@ FLOPS = 2 * TOKENS * FEATURES * (BOTTLENECK + FEATURES)
 
 def tile_splatinformationflow_kernel(tc, splat, dec_w, dec_b, tok, gate_w, gate_b, offs, out):
     nc = tc.nc
-    output_tiles = [(piece, block) for piece in range(PIECES) for block in range(BLOCKS)]
 
     with (
         tc.tile_pool(name="held", bufs=1) as held,
-        tc.tile_pool(name="work", bufs=len(output_tiles)) as work,
+        tc.tile_pool(name="work", bufs=PIECES * BLOCKS) as work,
         tc.psum_pool(name="psum", bufs=PSUM_BANKS) as psum,
     ):
         queues = [nc.sync, nc.scalar]
@@ -49,13 +50,15 @@ def tile_splatinformationflow_kernel(tc, splat, dec_w, dec_b, tok, gate_w, gate_
             loads.append((gate_w_sb[half], gate_w[half * P : (half + 1) * P, :]))
             loads.append((tok_sb[0][half], tok_part(0, half)))
         loads.append((gate_b_sb, gate_b.rearrange("(block p) one -> p (block one)", p=P)))
-        for piece in range(1, PIECES):
+        for piece in range(1, LAST_PIECE):
             for half in range(HALVES):
                 loads.append((tok_sb[piece][half], tok_part(piece, half)))
         loads.append((dec_w_sb, dec_w))
         loads.append((offsets, offs))
         loads.append((table, splat))
         loads.append((dec_b_sb, dec_b.rearrange("(block p) one -> p (block one)", p=P)))
+        for half in range(HALVES):
+            loads.append((tok_sb[LAST_PIECE][half], tok_part(LAST_PIECE, half)))
         with nc.allow_non_contiguous_dma(reason="the bias vectors: one element to a partition"):
             for position, (destination, source) in enumerate(loads):
                 queues[position % len(queues)].dma_start(destination[:], source)
@@ -67,25 +70,13 @@ def tile_splatinformationflow_kernel(tc, splat, dec_w, dec_b, tok, gate_w, gate_
             nc.tensor.matmul(warm_acc[:], zeros[:], zeros[:], start=True, stop=True)
 
         gates = {}
-        for piece in range(PIECES):
-            gate_accs = [psum.tile([P, PIECE], F32, name=f"gate_acc_block{block}", tag="bank") for block in range(BLOCKS)]
-            for half in range(HALVES):
-                for block in range(BLOCKS):
-                    nc.tensor.matmul(
-                        gate_accs[block][:],
-                        gate_w_sb[half][:, block * P : (block + 1) * P],
-                        tok_sb[piece][half][:],
-                        start=(half == 0),
-                        stop=(half == HALVES - 1),
-                    )
-            for block in range(BLOCKS):
-                gate = work.tile([P, PIECE], F32, name="gate")
-                nc.scalar.activation(
-                    gate[:], gate_accs[block][:], SIGMOID, bias=gate_b_sb[:, block : block + 1], scale=1.0
-                )
-                gates[piece, block] = gate
 
-        for piece, block in output_tiles:
+        def squash(piece, block, gate_acc):
+            gate = work.tile([P, PIECE], F32, name="gate")
+            nc.scalar.activation(gate[:], gate_acc[:], SIGMOID, bias=gate_b_sb[:, block : block + 1], scale=1.0)
+            gates[piece, block] = gate
+
+        def finish(piece, block):
             piece_offsets = offsets[:, piece * PIECE_OFFSET_COLUMNS : (piece + 1) * PIECE_OFFSET_COLUMNS]
             flow_acc = psum.tile([P, PIECE], F32, name="flow_acc", tag="bank")
             nc.tensor.matmul(
@@ -100,3 +91,37 @@ def tile_splatinformationflow_kernel(tc, splat, dec_w, dec_b, tok, gate_w, gate_
                 result[:], flow_acc[:], dec_b_sb[:, block : block + 1], gates[piece, block][:], ADD, MULT
             )
             nc.sync.dma_start(out[block * P : (block + 1) * P, piece * PIECE : (piece + 1) * PIECE], result[:])
+
+        for piece in range(LAST_PIECE):
+            gate_accs = [psum.tile([P, PIECE], F32, name=f"gate_acc_block{block}", tag="bank") for block in range(BLOCKS)]
+            for half in range(HALVES):
+                for block in range(BLOCKS):
+                    nc.tensor.matmul(
+                        gate_accs[block][:],
+                        gate_w_sb[half][:, block * P : (block + 1) * P],
+                        tok_sb[piece][half][:],
+                        start=(half == 0),
+                        stop=(half == HALVES - 1),
+                    )
+            for block in range(BLOCKS):
+                squash(piece, block, gate_accs[block])
+
+        for piece in range(LAST_PIECE):
+            for block in range(BLOCKS):
+                finish(piece, block)
+
+        for block in range(BLOCKS):
+            gate_acc = psum.tile([P, PIECE], F32, name="gate_acc_last", tag="bank")
+            for chunk in range(0, PIECE, CHUNK):
+                for half in range(HALVES):
+                    nc.tensor.matmul(
+                        gate_acc[:, chunk : chunk + CHUNK],
+                        gate_w_sb[half][:, block * P : (block + 1) * P],
+                        tok_sb[LAST_PIECE][half][:, chunk : chunk + CHUNK],
+                        start=(half == 0),
+                        stop=(half == HALVES - 1),
+                    )
+            squash(LAST_PIECE, block, gate_acc)
+
+        for block in range(BLOCKS):
+            finish(LAST_PIECE, block)

import concourse.mybir as mybir

BF16, F32, U16 = mybir.dt.bfloat16, mybir.dt.float32, mybir.dt.uint16
ADD, MULT = mybir.AluOpType.add, mybir.AluOpType.mult
SIGMOID = mybir.ActivationFunctionType.Sigmoid

P = 128
BOTTLENECK = 128
SPLATS = 1024
FEATURES = 256
TOKENS = 2048
PIECE = 512
BLOCKS = FEATURES // P
HALVES = FEATURES // P
PIECES = TOKENS // PIECE
LAST_PIECE = PIECES - 1
PIECE_OFFSET_COLUMNS = PIECE // 16
PSUM_BANKS = 8
CHUNK = 64
WARMUP_MATMULS = 8

FLOPS = 2 * TOKENS * FEATURES * (BOTTLENECK + FEATURES)


def tile_splatinformationflow_kernel(tc, splat, dec_w, dec_b, tok, gate_w, gate_b, offs, out):
    nc = tc.nc

    with (
        tc.tile_pool(name="held", bufs=1) as held,
        tc.tile_pool(name="work", bufs=PIECES * BLOCKS) as work,
        tc.psum_pool(name="psum", bufs=PSUM_BANKS) as psum,
    ):
        queues = [nc.sync, nc.scalar]
        gate_w_sb = [held.tile([P, FEATURES], BF16, name=f"gate_w_half{half}") for half in range(HALVES)]
        tok_sb = [
            [held.tile([P, PIECE], BF16, name=f"tok_piece{piece}_half{half}") for half in range(HALVES)]
            for piece in range(PIECES)
        ]
        gate_b_sb = held.tile([P, BLOCKS], F32, name="gate_b_sb")
        dec_b_sb = held.tile([P, BLOCKS], F32, name="dec_b_sb")
        table = held.tile([BOTTLENECK, SPLATS], BF16, name="table")
        dec_w_sb = held.tile([BOTTLENECK, FEATURES], BF16, name="dec_w_sb")
        offsets = held.tile([P, TOKENS // 16], U16, name="offsets")

        def tok_part(piece, half):
            return tok[half * P : (half + 1) * P, piece * PIECE : (piece + 1) * PIECE]

        loads = []
        for half in range(HALVES):
            loads.append((gate_w_sb[half], gate_w[half * P : (half + 1) * P, :]))
            loads.append((tok_sb[0][half], tok_part(0, half)))
        loads.append((gate_b_sb, gate_b.rearrange("(block p) one -> p (block one)", p=P)))
        for piece in range(1, LAST_PIECE):
            for half in range(HALVES):
                loads.append((tok_sb[piece][half], tok_part(piece, half)))
        loads.append((dec_w_sb, dec_w))
        loads.append((offsets, offs))
        loads.append((table, splat))
        loads.append((dec_b_sb, dec_b.rearrange("(block p) one -> p (block one)", p=P)))
        for half in range(HALVES):
            loads.append((tok_sb[LAST_PIECE][half], tok_part(LAST_PIECE, half)))
        with nc.allow_non_contiguous_dma(reason="the bias vectors: one element to a partition"):
            for position, (destination, source) in enumerate(loads):
                queues[position % len(queues)].dma_start(destination[:], source)

        zeros = held.tile([P, P], BF16, name="zeros")
        nc.vector.memset(zeros[:], 0.0)
        warm_acc = psum.tile([P, P], F32, name="warm_acc", tag="bank")
        for repeat in range(WARMUP_MATMULS):
            nc.tensor.matmul(warm_acc[:], zeros[:], zeros[:], start=True, stop=True)

        gates = {}

        def squash(piece, block, gate_acc):
            gate = work.tile([P, PIECE], F32, name="gate")
            nc.scalar.activation(gate[:], gate_acc[:], SIGMOID, bias=gate_b_sb[:, block : block + 1], scale=1.0)
            gates[piece, block] = gate

        def finish(piece, block):
            piece_offsets = offsets[:, piece * PIECE_OFFSET_COLUMNS : (piece + 1) * PIECE_OFFSET_COLUMNS]
            flow_acc = psum.tile([P, PIECE], F32, name="flow_acc", tag="bank")
            nc.tensor.matmul(
                flow_acc[:],
                dec_w_sb[:, block * P : (block + 1) * P],
                table[:].indirect(piece_offsets),
                start=True,
                stop=True,
            )
            result = work.tile([P, PIECE], F32, name="result")
            nc.vector.scalar_tensor_tensor(
                result[:], flow_acc[:], dec_b_sb[:, block : block + 1], gates[piece, block][:], ADD, MULT
            )
            nc.sync.dma_start(out[block * P : (block + 1) * P, piece * PIECE : (piece + 1) * PIECE], result[:])

        for piece in range(LAST_PIECE):
            gate_accs = [psum.tile([P, PIECE], F32, name=f"gate_acc_block{block}", tag="bank") for block in range(BLOCKS)]
            for half in range(HALVES):
                for block in range(BLOCKS):
                    nc.tensor.matmul(
                        gate_accs[block][:],
                        gate_w_sb[half][:, block * P : (block + 1) * P],
                        tok_sb[piece][half][:],
                        start=(half == 0),
                        stop=(half == HALVES - 1),
                    )
            for block in range(BLOCKS):
                squash(piece, block, gate_accs[block])

        for piece in range(LAST_PIECE):
            for block in range(BLOCKS):
                finish(piece, block)

        for block in range(BLOCKS):
            gate_acc = psum.tile([P, PIECE], F32, name="gate_acc_last", tag="bank")
            for chunk in range(0, PIECE, CHUNK):
                for half in range(HALVES):
                    nc.tensor.matmul(
                        gate_acc[:, chunk : chunk + CHUNK],
                        gate_w_sb[half][:, block * P : (block + 1) * P],
                        tok_sb[LAST_PIECE][half][:, chunk : chunk + CHUNK],
                        start=(half == 0),
                        stop=(half == HALVES - 1),
                    )
            squash(LAST_PIECE, block, gate_acc)

        for block in range(BLOCKS):
            finish(LAST_PIECE, block)
